import numpy as np
import ml_dtypes


def mxq(x, axis, fmt="e4m3"):
    dtype, down = {"e4m3": (ml_dtypes.float8_e4m3fn, 7), "e5m2": (ml_dtypes.float8_e5m2, 14)}[fmt]
    v = np.moveaxis(np.asarray(x, np.float32).astype(ml_dtypes.bfloat16).astype(np.float64), axis, -1)
    blocks = v.reshape(v.shape[:-1] + (-1, 32))
    amax = np.abs(blocks).max(-1, keepdims=True)
    byte = np.maximum(np.where(amax > 0, np.frexp(amax)[1] - 1 + 127, 0) - down, 1)
    scale = np.exp2(byte - 127.0)
    codes = (blocks / scale).astype(np.float32).astype(dtype).astype(np.float64)
    return np.moveaxis((codes * scale).reshape(v.shape), -1, axis)


WIDE = False


def mx_kscale(k):
    if not WIDE:
        return np.ones(k)
    levels = np.array([10, -10, 5, -5, 0])
    a = np.random.permutation(np.resize(levels, k // 512 * 4)).reshape(k // 512, 4)
    idx = np.arange(k)
    return np.exp2(a[idx // 512, idx % 128 // 32])


BF16 = ml_dtypes.bfloat16


def bf(x):
    return np.asarray(x, np.float32).astype(BF16)


def f64(x):
    return np.asarray(x).astype(np.float64)


E2M1 = np.array([0.0, 0.5, 1.0, 1.5, 2.0, 3.0, 4.0, 6.0, -0.0, -0.5, -1.0, -1.5, -2.0, -3.0, -4.0, -6.0])


def pack_weight(w, fmt):
    k, n = w.shape
    w = f64(bf(w)).reshape(k // 32, 32, n)
    amax = np.abs(w).max(1)
    if fmt == "e4m3":
        byte = np.frexp(amax)[1] - 1 + 127 - 7
    else:
        mant, ex = np.frexp(amax / 6.0)
        byte = np.where(mant > 0.5, ex, ex - 1) + 127
    byte = np.clip(np.where(amax > 0, byte, 1), 1, 254)
    scaled = (w * np.exp2(127.0 - byte)[:, None, :]).reshape(k, n).astype(np.float32)
    by_word = np.ascontiguousarray(scaled.reshape(k // 512, 128, 4, n).transpose(0, 1, 3, 2))
    if fmt == "e4m3":
        words = by_word.astype(ml_dtypes.float8_e4m3fn).view(np.uint8)
    else:
        c = by_word.astype(ml_dtypes.float4_e2m1fn).view(np.uint8) & 0xF
        words = c[..., 0::2] | (c[..., 1::2] << 4)
    return np.ascontiguousarray(words), np.ascontiguousarray(byte.astype(np.uint8).reshape(k // 512, 16, n))


def unpack_weight(words, scales, fmt):
    g, p, n, _ = words.shape
    if fmt == "e4m3":
        vals = np.ascontiguousarray(words).view(ml_dtypes.float8_e4m3fn).astype(np.float64)
    else:
        nib = np.empty((g, p, n, 4), np.uint8)
        nib[..., 0::2] = words & 0xF
        nib[..., 1::2] = words >> 4
        vals = E2M1[nib]
    vals = vals * np.repeat(np.exp2(scales.astype(np.float64) - 127.0), 8, axis=1)[..., None]
    return vals.transpose(0, 1, 3, 2).reshape(g * 512, n)


B, N, C, DIM, H = 4, 128, 2048, 2048, 16
D = DIM // H // 2
LAYER_NUM = 12
LAM_INIT = 0.8 - 0.6 * np.exp(-0.3 * LAYER_NUM)
EPS = 1e-5
FMT = "e4m3"


def setup_inputs():
    s = mx_kscale(C)
    sc = np.random.standard_normal((B, N, 2 * H, 2 * H))
    att = np.exp(sc) / np.exp(sc).sum(-1, keepdims=True)
    diff = att[:, :, :H, :H] - LAM_INIT * att[:, :, H:, H:]
    x = bf(np.random.standard_normal((B, N, C)) * s)
    Wv = np.random.standard_normal((DIM, C)) * 0.02 * np.sqrt(H / C) / s
    Wv_words, Wv_scales = pack_weight(Wv.T, FMT)
    Wo = np.random.standard_normal((C, DIM)) * 2.0 / np.sqrt(DIM)
    Wo_words, Wo_scales = pack_weight(Wo.T, FMT)
    bo = bf(np.random.standard_normal(C) * 0.1)
    return {"x": x,
            "diff": bf(diff),
            "Wv_words": Wv_words,
            "Wv_scales": Wv_scales,
            "Wo_words": Wo_words,
            "Wo_scales": Wo_scales,
            "bo": bo}


def reference(x, diff, Wv_words, Wv_scales, Wo_words, Wo_scales, bo):
    v = (mxq(f64(x), 2, "e4m3") @ unpack_weight(Wv_words, Wv_scales, FMT)).reshape(B, N, H, 2 * D)
    w = f64(diff)
    out = sum(w[:, :, :, h:h + 1] * v[:, :, h:h + 1, :] for h in range(H))
    out = out * (1.0 / np.sqrt(np.mean(out * out, axis=-1, keepdims=True) + EPS))
    out = out * (1.0 - LAM_INIT)
    out = out.reshape(B, N, DIM)
    return (mxq(out, 2, "e4m3") @ unpack_weight(Wo_words, Wo_scales, FMT)) + f64(bo)

@@ -1,0 +1,311 @@
+import math
+from contextlib import ExitStack
+
+import concourse.mybir as mybir
+from concourse.masks import make_identity
+
+F32 = mybir.dt.float32
+BF16 = mybir.dt.bfloat16
+I32 = mybir.dt.int32
+U32 = mybir.dt.uint32
+U8 = mybir.dt.uint8
+FP8X4 = mybir.dt.float8_e4m3fn_x4
+ACT = mybir.ActivationFunctionType
+ALU = mybir.AluOpType
+
+P = 128
+PACK = 4
+PASSES = 4
+TOKENS = 512
+WIDTH = 2048
+HEADS = 16
+HEAD_DIM = 128
+CHUNK = 512
+N_CHUNKS = WIDTH // CHUNK
+TOKEN_TILES = TOKENS // P
+
+GROUP_TOKENS = 8
+GROUPS = TOKENS // GROUP_TOKENS
+GROUPS_PER_BANK = CHUNK // HEAD_DIM
+BANKS = GROUPS // GROUPS_PER_BANK
+BANKS_PER_TILE = BANKS // TOKEN_TILES
+GROUPS_PER_TILE = GROUPS // TOKEN_TILES
+
+L0 = 0.8 - 0.6 * math.exp(-0.3 * 12)
+KEEP = 1.0 - L0
+EPS = 1e-5
+
+FLOPS = 2 * 2 * TOKENS * WIDTH * WIDTH + 2 * TOKENS * HEADS * HEADS * HEAD_DIM
+
+
+def tile_differentialattention_pb_kernel(
+    tc, x, diff, Wv_words, Wv_scales, Wo_words, Wo_scales, bo, out
+):
+    nc = tc.nc
+    x_rows = x.flatten_outer_dims()
+    out_rows = out.flatten_outer_dims()
+
+    with ExitStack() as ctx:
+        const = ctx.enter_context(tc.tile_pool(name="const", bufs=1))
+        keep = ctx.enter_context(tc.tile_pool(name="keep", bufs=1))
+        weights = ctx.enter_context(tc.tile_pool(name="weights", bufs=N_CHUNKS))
+        work = ctx.enter_context(tc.tile_pool(name="work", bufs=3))
+        stats = ctx.enter_context(tc.tile_pool(name="stats", bufs=4))
+        psum_t = ctx.enter_context(tc.psum_pool(name="psum_t", bufs=2))
+        psum_acc = ctx.enter_context(tc.psum_pool(name="psum_acc", bufs=3))
+        psum_mix = ctx.enter_context(tc.psum_pool(name="psum_mix", bufs=3))
+
+        ident_f32 = const.tile([P, P], F32)
+        make_identity(nc, ident_f32[:])
+        ident_bf16 = const.tile([P, P], BF16)
+        make_identity(nc, ident_bf16[:])
+
+        one = const.tile([P, 1], F32)
+        nc.vector.memset(one[:], 1.0)
+        one_root = const.tile([P, 1], F32)
+        nc.scalar.activation(out=one_root[:], in_=one[:], func=ACT.Sqrt)
+
+        same_token = const.tile([P, GROUP_TOKENS], F32)
+        nc.vector.tensor_reduce(
+            out=same_token[:],
+            in_=ident_f32[:].rearrange("k (t h) -> k t h", h=HEADS),
+            axis=mybir.AxisListType.X,
+            op=ALU.add,
+        )
+
+        x_sb = keep.tile([P, TOKEN_TILES, WIDTH], BF16)
+        for c in range(TOKEN_TILES):
+            nc.sync.dma_start(out=x_sb[:, c, :], in_=x_rows[c * P : (c + 1) * P, :])
+
+        def load_scale_planes(scales, name):
+            planes = const.tile([P, WIDTH], U8, name=name, align_bytes=64)
+            nc.vector.memset(planes[:].bitcast(I32), 0)
+            rows = scales.bitcast(I32)
+            for quadrant in range(4):
+                nc.sync.dma_start(
+                    out=planes[32 * quadrant : 32 * quadrant + 16, :].bitcast(I32),
+                    in_=rows[:, 4 * quadrant : 4 * quadrant + 4, :],
+                )
+            return planes
+
+        def load_weight_chunk(words, chunk):
+            view = words.rearrange("g p n j -> g p (n j)").bitcast(I32).rearrange("g p n -> p g n")
+            w = weights.tile([P, PASSES, CHUNK], U32, tag="w", align_bytes=64)
+            nc.sync.dma_start(
+                out=w[:].bitcast(I32), in_=view[:, :, chunk * CHUNK : (chunk + 1) * CHUNK]
+            )
+            return w
+
+        wv_planes = load_scale_planes(Wv_scales, "wv_planes")
+        wv = [load_weight_chunk(Wv_words, 0), load_weight_chunk(Wv_words, 1)]
+
+        diff_rows = keep.tile([P, 8, GROUP_TOKENS, HEADS], BF16)
+        diff_view = diff.rearrange("b n a h -> (b n) a h").rearrange(
+            "(t c l) a h -> (l a) c t h", t=GROUP_TOKENS, c=8, l=8
+        )
+        for c in range(8):
+            nc.sync.dma_start(out=diff_rows[:, c, :, :], in_=diff_view[:, c, :, :])
+
+        wv.append(load_weight_chunk(Wv_words, 2))
+        wv.append(load_weight_chunk(Wv_words, 3))
+
+        bias = const.tile([P, WIDTH], BF16)
+        nc.sync.dma_start(out=bias[:], in_=bo.partition_broadcast(P))
+        wo_planes = load_scale_planes(Wo_scales, "wo_planes")
+
+        x_grouped = keep.tile([P, PASSES, TOKENS, PACK], BF16, align_bytes=64)
+        x_grouped_words = (
+            x_grouped[:]
+            .rearrange("p g t j -> p (g t j)")
+            .bitcast(F32)
+            .rearrange("p (g t u) -> p g t u", g=PASSES, u=2)
+        )
+        for c in range(TOKEN_TILES):
+            x_words = x_sb[:, c, :].bitcast(F32)
+            for half in range(2):
+                xt = psum_t.tile([P, 2, 2, P], F32, tag="t")
+                for gi in range(2):
+                    g = 2 * half + gi
+                    for u in range(2):
+                        nc.tensor.transpose(
+                            xt[:, gi, u, :], x_words[:, 256 * g + u : 256 * (g + 1) : 2], ident_f32[:]
+                        )
+                copy = nc.vector.tensor_copy if half == 0 else nc.scalar.copy
+                copy(
+                    out=x_grouped_words[:, 2 * half : 2 * half + 2, c * P : (c + 1) * P, :],
+                    in_=xt[:].rearrange("p g u t -> p g t u"),
+                )
+
+        x_codes = keep.tile([P, PASSES, TOKENS], U32, align_bytes=64)
+        x_scales = keep.tile([P, PASSES, TOKENS], U8, align_bytes=64)
+        for g in range(PASSES):
+            nc.vector.quantize_mx(
+                out=x_codes[:, g, :].bitcast(FP8X4),
+                scales=x_scales[:, g, :],
+                in_=x_grouped[:, g, :, :].rearrange("p t j -> p (t j)"),
+            )
+
+        v_t = keep.tile([P, GROUP_TOKENS, HEADS, GROUPS], F32)
+        wo = []
+
+        def first_product(head):
+            w = wv[head // 4]
+            cols = slice((head % 4) * P, (head % 4 + 1) * P)
+            acc = psum_acc.tile([P, TOKENS], F32, tag="acc")
+            for g in range(PASSES):
+                nc.tensor.matmul_mx(
+                    out=acc[:],
+                    lhsT=w[:, g, cols].bitcast(FP8X4),
+                    lhsT_scale=wv_planes[4 * g : P, head * P : (head + 1) * P],
+                    rhs=x_codes[:, g, :].bitcast(FP8X4),
+                    rhs_scale=x_scales[:, g, :],
+                    start=(g == 0),
+                    stop=(g == PASSES - 1),
+                )
+            copy = nc.scalar.copy if head % 2 == 0 else nc.vector.tensor_copy
+            copy(out=v_t[:, :, head, :], in_=acc[:].rearrange("d (t a) -> d t a", a=GROUPS))
+
+        mixer = keep.tile([P, GROUPS, HEADS, GROUP_TOKENS], F32)
+
+        def build_mixer():
+            diff_tp = psum_t.tile([P, 8, P], BF16, tag="t")
+            for c in range(8):
+                nc.tensor.transpose(
+                    diff_tp[:, c, :],
+                    diff_rows[:, c, :, :].rearrange("q t h -> q (t h)"),
+                    ident_bf16[:],
+                )
+            diff_t = keep.tile([P, GROUPS, 4, 4], F32)
+            nc.vector.tensor_copy(
+                out=diff_t[:],
+                in_=diff_tp[:].rearrange("k c (l hi lo) -> k (c l) lo hi", l=8, hi=4, lo=4),
+            )
+            for tile_index in range(TOKEN_TILES):
+                groups = slice(tile_index * GROUPS_PER_TILE, (tile_index + 1) * GROUPS_PER_TILE)
+                shape = [P, GROUPS_PER_TILE * HEADS, GROUP_TOKENS]
+                nc.vector.tensor_tensor(
+                    out=mixer[:, groups, :, :].rearrange("k a m t -> k (a m) t"),
+                    in0=diff_t[:, groups, :, :]
+                    .rearrange("k a lo hi -> k (a lo hi)")
+                    .unsqueeze(2)
+                    .to_broadcast(shape),
+                    in1=same_token[:].unsqueeze(1).to_broadcast(shape),
+                    op=ALU.mult,
+                )
+
+        for head in range(HEADS):
+            first_product(head)
+            if head % 4 == 3:
+                wo.append(load_weight_chunk(Wo_words, head // 4))
+            if head == HEADS // 2 - 1:
+                build_mixer()
+
+        r_codes = keep.tile([P, TOKEN_TILES, PASSES * P], U32, align_bytes=64)
+        r_scales = keep.tile([P, TOKEN_TILES, PASSES * P], U8, align_bytes=64)
+        v_t_columns = v_t[:].rearrange("d t h a -> d (t h) a")
+        v_groups = {}
+        r_grouped = {}
+
+        def transpose_v(bank):
+            v_tp = psum_t.tile([P, GROUPS_PER_BANK, HEAD_DIM], F32, tag="t")
+            for i in range(GROUPS_PER_BANK):
+                nc.tensor.transpose(
+                    v_tp[:, i, :], v_t_columns[:, :, bank * GROUPS_PER_BANK + i], ident_f32[:]
+                )
+            v_g = work.tile([P, GROUPS_PER_BANK, PACK, 32], F32, tag="v_g")
+            nc.scalar.copy(out=v_g[:], in_=v_tp[:].rearrange("k i (q j) -> k i j q", j=PACK))
+            v_groups[bank] = v_g
+
+        def mix_and_norm(bank):
+            tile_index, bank_in_tile = divmod(bank, BANKS_PER_TILE)
+            v_g = v_groups[bank]
+            mixed = psum_mix.tile([P, GROUPS_PER_BANK, HEAD_DIM], F32, tag="mix")
+            for i in range(GROUPS_PER_BANK):
+                nc.tensor.matmul(
+                    out=mixed[:, i, :],
+                    lhsT=mixer[:, bank * GROUPS_PER_BANK + i, :, :].rearrange("k m t -> k (m t)"),
+                    rhs=v_g[:, i, :, :].rearrange("k j q -> k (j q)"),
+                    start=True,
+                    stop=True,
+                )
+            squares = work.tile([P, GROUPS_PER_BANK, HEAD_DIM], BF16, tag="squares")
+            sum_sq = stats.tile([P, GROUPS_PER_BANK], F32, tag="sum_sq")
+            for i in range(GROUPS_PER_BANK):
+                nc.scalar.activation(
+                    out=squares[:, i, :],
+                    in_=mixed[:, i, :],
+                    func=ACT.Square,
+                    accum_out=sum_sq[:, i : i + 1],
+                )
+            root = stats.tile([P, GROUPS_PER_BANK], F32, tag="root")
+            nc.scalar.activation(
+                out=root[:],
+                in_=sum_sq[:],
+                func=ACT.Sqrt,
+                scale=1.0 / (HEAD_DIM * KEEP * KEEP),
+                bias=EPS / (KEEP * KEEP),
+            )
+            gain = stats.tile([P, GROUPS_PER_BANK], F32, tag="gain")
+            nc.vector.reciprocal(out=gain[:], in_=root[:])
+            r_rows = work.tile([P, GROUPS_PER_BANK, HEAD_DIM], BF16, tag="r_rows", align_bytes=64)
+            nc.vector.tensor_tensor(
+                out=r_rows[:],
+                in0=mixed[:],
+                in1=gain[:].unsqueeze(2).to_broadcast([P, GROUPS_PER_BANK, HEAD_DIM]),
+                op=ALU.mult,
+            )
+            r_cols = work.tile([P, CHUNK], BF16, tag="r_cols", align_bytes=64)
+            nc.vector.transpose(out=r_cols[:], in_=r_rows[:].rearrange("m i c -> m (i c)"))
+            if bank_in_tile == 0:
+                r_grouped[tile_index] = work.tile(
+                    [P, PASSES, GROUPS_PER_TILE, GROUP_TOKENS, PACK],
+                    BF16,
+                    name="r_grouped",
+                    tag="r_grouped",
+                    bufs=2,
+                    align_bytes=64,
+                )
+            first = bank_in_tile * GROUPS_PER_BANK
+            nc.vector.tensor_copy(
+                out=r_grouped[tile_index][:, :, first : first + GROUPS_PER_BANK, :, :],
+                in_=r_cols[:].rearrange(
+                    "p (a j hi t) -> p hi a t j", a=GROUPS_PER_BANK, j=PACK, hi=PASSES
+                ),
+            )
+            if bank_in_tile == BANKS_PER_TILE - 1:
+                nc.vector.quantize_mx(
+                    out=r_codes[:, tile_index, :].bitcast(FP8X4),
+                    scales=r_scales[:, tile_index, :],
+                    in_=r_grouped[tile_index][:].rearrange("p g a t j -> p (g a t j)"),
+                )
+
+        out_view = out_rows.rearrange(
+            "(t i a) n -> i a t n", t=GROUP_TOKENS, i=TOKEN_TILES, a=GROUPS_PER_TILE
+        )
+
+        def second_product(tile_index):
+            for chunk in range(N_CHUNKS):
+                cols = slice(chunk * CHUNK, (chunk + 1) * CHUNK)
+                acc = psum_acc.tile([P, CHUNK], F32, tag="acc")
+                for g in range(PASSES):
+                    nc.tensor.matmul_mx(
+                        out=acc[:],
+                        lhsT=r_codes[:, tile_index, g * P : (g + 1) * P].bitcast(FP8X4),
+                        lhsT_scale=r_scales[:, tile_index, g * P : (g + 1) * P],
+                        rhs=wo[chunk][:, g, :].bitcast(FP8X4),
+                        rhs_scale=wo_planes[4 * g : P, cols],
+                        start=(g == 0),
+                        stop=(g == PASSES - 1),
+                    )
+                result = work.tile([P, CHUNK], F32, tag="result")
+                nc.vector.tensor_tensor(out=result[:], in0=acc[:], in1=bias[:, cols], op=ALU.add)
+                nc.sync.dma_start(out=out_view[tile_index][:, :, cols], in_=result[:])
+
+        transpose_v(0)
+        for bank in range(BANKS):
+            if bank + 1 < BANKS:
+                transpose_v(bank + 1)
+            mix_and_norm(bank)
+            if bank % BANKS_PER_TILE == BANKS_PER_TILE - 1 and bank >= 2 * BANKS_PER_TILE - 1:
+                second_product(bank // BANKS_PER_TILE - 1)
+        second_product(TOKEN_TILES - 1)

@@ -54,6 +54,7 @@ def tile_differentialattention_pb_kernel(
         psum_t = ctx.enter_context(tc.psum_pool(name="psum_t", bufs=2))
         psum_acc = ctx.enter_context(tc.psum_pool(name="psum_acc", bufs=3))
         psum_mix = ctx.enter_context(tc.psum_pool(name="psum_mix", bufs=3))
+        ctx.enter_context(tc.manual_schedule())
 
         ident_f32 = const.tile([P, P], F32)
         make_identity(nc, ident_f32[:])
@@ -68,14 +69,20 @@ def tile_differentialattention_pb_kernel(
         same_token = const.tile([P, GROUP_TOKENS], F32)
         nc.vector.tensor_reduce(
             out=same_token[:],
-            in_=ident_f32[:].rearrange("k (t h) -> k t h", h=HEADS),
+            in_=ident_f32[:].rearrange("k (h t) -> k t h", h=HEADS),
             axis=mybir.AxisListType.X,
             op=ALU.add,
         )
 
+        x_view = x_rows.rearrange(
+            "(t i a) k -> i a t k", t=GROUP_TOKENS, i=TOKEN_TILES, a=GROUPS_PER_TILE
+        )
+        out_view = out_rows.rearrange(
+            "(t i a) n -> i a t n", t=GROUP_TOKENS, i=TOKEN_TILES, a=GROUPS_PER_TILE
+        )
         x_sb = keep.tile([P, TOKEN_TILES, WIDTH], BF16)
         for c in range(TOKEN_TILES):
-            nc.sync.dma_start(out=x_sb[:, c, :], in_=x_rows[c * P : (c + 1) * P, :])
+            nc.sync.dma_start(out=x_sb[:, c, :], in_=x_view[c])
 
         def load_scale_planes(scales, name):
             planes = const.tile([P, WIDTH], U8, name=name, align_bytes=64)
@@ -145,7 +152,7 @@ def tile_differentialattention_pb_kernel(
                 in_=x_grouped[:, g, :, :].rearrange("p t j -> p (t j)"),
             )
 
-        v_t = keep.tile([P, GROUP_TOKENS, HEADS, GROUPS], F32)
+        v_t = keep.tile([P, GROUPS, HEADS, GROUP_TOKENS], F32)
         wo = []
 
         def first_product(head):
@@ -162,17 +169,20 @@ def tile_differentialattention_pb_kernel(
                     start=(g == 0),
                     stop=(g == PASSES - 1),
                 )
-            copy = nc.scalar.copy if head % 2 == 0 else nc.vector.tensor_copy
-            copy(out=v_t[:, :, head, :], in_=acc[:].rearrange("d (t a) -> d t a", a=GROUPS))
+            nc.scalar.copy(
+                out=v_t[:, :, head, :], in_=acc[:].rearrange("d (a t) -> d a t", t=GROUP_TOKENS)
+            )
 
         mixer = keep.tile([P, GROUPS, HEADS, GROUP_TOKENS], F32)
 
         def build_mixer():
+            diff_cols = keep.tile([P, 8, HEADS, GROUP_TOKENS], BF16)
+            nc.vector.tensor_copy(out=diff_cols[:], in_=diff_rows[:].rearrange("q c t h -> q c h t"))
             diff_tp = psum_t.tile([P, 8, P], BF16, tag="t")
             for c in range(8):
                 nc.tensor.transpose(
                     diff_tp[:, c, :],
-                    diff_rows[:, c, :, :].rearrange("q t h -> q (t h)"),
+                    diff_cols[:, c, :, :].rearrange("q h t -> q (h t)"),
                     ident_bf16[:],
                 )
             diff_t = keep.tile([P, GROUPS, 4, 4], F32)
@@ -202,7 +212,6 @@ def tile_differentialattention_pb_kernel(
 
         r_codes = keep.tile([P, TOKEN_TILES, PASSES * P], U32, align_bytes=64)
         r_scales = keep.tile([P, TOKEN_TILES, PASSES * P], U8, align_bytes=64)
-        v_t_columns = v_t[:].rearrange("d t h a -> d (t h) a")
         v_groups = {}
         r_grouped = {}
 
@@ -210,7 +219,9 @@ def tile_differentialattention_pb_kernel(
             v_tp = psum_t.tile([P, GROUPS_PER_BANK, HEAD_DIM], F32, tag="t")
             for i in range(GROUPS_PER_BANK):
                 nc.tensor.transpose(
-                    v_tp[:, i, :], v_t_columns[:, :, bank * GROUPS_PER_BANK + i], ident_f32[:]
+                    v_tp[:, i, :],
+                    v_t[:, bank * GROUPS_PER_BANK + i, :, :].rearrange("d h t -> d (h t)"),
+                    ident_f32[:],
                 )
             v_g = work.tile([P, GROUPS_PER_BANK, PACK, 32], F32, tag="v_g")
             nc.scalar.copy(out=v_g[:], in_=v_tp[:].rearrange("k i (q j) -> k i j q", j=PACK))
@@ -278,10 +289,6 @@ def tile_differentialattention_pb_kernel(
                     scales=r_scales[:, tile_index, :],
                     in_=r_grouped[tile_index][:].rearrange("p g a t j -> p (g a t j)"),
                 )
-
-        out_view = out_rows.rearrange(
-            "(t i a) n -> i a t n", t=GROUP_TOKENS, i=TOKEN_TILES, a=GROUPS_PER_TILE
-        )
 
         def second_product(tile_index):
             for chunk in range(N_CHUNKS):

@@ -20,16 +20,20 @@ TOKENS = 512
 WIDTH = 2048
 HEADS = 16
 HEAD_DIM = 128
-CHUNK = 512
-N_CHUNKS = WIDTH // CHUNK
+BANK = 512
+PSUM_BANKS = 8
+N_CHUNKS = WIDTH // BANK
 TOKEN_TILES = TOKENS // P
+HALF = TOKENS // 2
+HEAD_PAIRS = HEADS // 2
 
 GROUP_TOKENS = 8
 GROUPS = TOKENS // GROUP_TOKENS
-GROUPS_PER_BANK = CHUNK // HEAD_DIM
-BANKS = GROUPS // GROUPS_PER_BANK
-BANKS_PER_TILE = BANKS // TOKEN_TILES
+GROUPS_PER_BANK = BANK // HEAD_DIM
+MIX_BANKS = GROUPS // GROUPS_PER_BANK
+BANKS_PER_TILE = MIX_BANKS // TOKEN_TILES
 GROUPS_PER_TILE = GROUPS // TOKEN_TILES
+STEPS = MIX_BANKS // 2
 
 L0 = 0.8 - 0.6 * math.exp(-0.3 * 12)
 KEEP = 1.0 - L0
@@ -48,13 +52,14 @@ def tile_differentialattention_pb_kernel(
     with ExitStack() as ctx:
         const = ctx.enter_context(tc.tile_pool(name="const", bufs=1))
         keep = ctx.enter_context(tc.tile_pool(name="keep", bufs=1))
-        weights = ctx.enter_context(tc.tile_pool(name="weights", bufs=N_CHUNKS))
-        work = ctx.enter_context(tc.tile_pool(name="work", bufs=3))
-        stats = ctx.enter_context(tc.tile_pool(name="stats", bufs=4))
-        psum_t = ctx.enter_context(tc.psum_pool(name="psum_t", bufs=2))
-        psum_acc = ctx.enter_context(tc.psum_pool(name="psum_acc", bufs=3))
-        psum_mix = ctx.enter_context(tc.psum_pool(name="psum_mix", bufs=3))
+        work = ctx.enter_context(tc.tile_pool(name="work", bufs=4))
+        psum = ctx.enter_context(tc.psum_pool(name="psum", bufs=PSUM_BANKS))
         ctx.enter_context(tc.manual_schedule())
+
+        wv_planes = const.tile([P, WIDTH], U8, align_bytes=64)
+        wo_planes = const.tile([P, WIDTH], U8, align_bytes=64)
+        nc.vector.memset(wv_planes[:].bitcast(I32), 0)
+        nc.vector.memset(wo_planes[:].bitcast(I32), 0)
 
         ident_f32 = const.tile([P, P], F32)
         make_identity(nc, ident_f32[:])
@@ -74,141 +79,136 @@ def tile_differentialattention_pb_kernel(
             op=ALU.add,
         )
 
-        x_view = x_rows.rearrange(
-            "(t i a) k -> i a t k", t=GROUP_TOKENS, i=TOKEN_TILES, a=GROUPS_PER_TILE
-        )
-        out_view = out_rows.rearrange(
-            "(t i a) n -> i a t n", t=GROUP_TOKENS, i=TOKEN_TILES, a=GROUPS_PER_TILE
-        )
-        x_sb = keep.tile([P, TOKEN_TILES, WIDTH], BF16)
-        for c in range(TOKEN_TILES):
-            nc.sync.dma_start(out=x_sb[:, c, :], in_=x_view[c])
+        x_sb = {}
 
-        def load_scale_planes(scales, name):
-            planes = const.tile([P, WIDTH], U8, name=name, align_bytes=64)
-            nc.vector.memset(planes[:].bitcast(I32), 0)
+        def load_x(tile_index):
+            x_sb[tile_index] = keep.tile([P, WIDTH], BF16, name="x_sb", tag="x_sb", bufs=2)
+            nc.sync.dma_start(
+                out=x_sb[tile_index][:], in_=x_rows[tile_index * P : (tile_index + 1) * P, :]
+            )
+
+        def load_scale_planes(planes, scales):
             rows = scales.bitcast(I32)
             for quadrant in range(4):
                 nc.sync.dma_start(
                     out=planes[32 * quadrant : 32 * quadrant + 16, :].bitcast(I32),
                     in_=rows[:, 4 * quadrant : 4 * quadrant + 4, :],
                 )
-            return planes
 
-        def load_weight_chunk(words, chunk):
+        def load_weight_columns(words, first, count, name):
             view = words.rearrange("g p n j -> g p (n j)").bitcast(I32).rearrange("g p n -> p g n")
-            w = weights.tile([P, PASSES, CHUNK], U32, tag="w", align_bytes=64)
-            nc.sync.dma_start(
-                out=w[:].bitcast(I32), in_=view[:, :, chunk * CHUNK : (chunk + 1) * CHUNK]
-            )
+            w = keep.tile([P, PASSES, count], U32, name=name, align_bytes=64)
+            nc.sync.dma_start(out=w[:].bitcast(I32), in_=view[:, :, first : first + count])
             return w
 
-        wv_planes = load_scale_planes(Wv_scales, "wv_planes")
-        wv = [load_weight_chunk(Wv_words, 0), load_weight_chunk(Wv_words, 1)]
+        def load_wv(pair):
+            return load_weight_columns(Wv_words, pair * 2 * HEAD_DIM, 2 * HEAD_DIM, "wv%d" % pair)
 
-        diff_rows = keep.tile([P, 8, GROUP_TOKENS, HEADS], BF16)
+        diff_rows = keep.tile([P, GROUP_TOKENS, 8, HEADS], BF16)
         diff_view = diff.rearrange("b n a h -> (b n) a h").rearrange(
-            "(t c l) a h -> (l a) c t h", t=GROUP_TOKENS, c=8, l=8
+            "(a t) (s e) h -> s a t (e h)", t=GROUP_TOKENS, s=2
         )
-        for c in range(8):
-            nc.sync.dma_start(out=diff_rows[:, c, :, :], in_=diff_view[:, c, :, :])
 
-        wv.append(load_weight_chunk(Wv_words, 2))
-        wv.append(load_weight_chunk(Wv_words, 3))
+        def load_diff():
+            for s in range(2):
+                nc.sync.dma_start(
+                    out=diff_rows[64 * s : 64 * (s + 1), :, :, :].rearrange("q t e h -> q t (e h)"),
+                    in_=diff_view[s],
+                )
 
         bias = const.tile([P, WIDTH], BF16)
-        nc.sync.dma_start(out=bias[:], in_=bo.partition_broadcast(P))
-        wo_planes = load_scale_planes(Wo_scales, "wo_planes")
-
-        x_grouped = keep.tile([P, PASSES, TOKENS, PACK], BF16, align_bytes=64)
-        x_grouped_words = (
-            x_grouped[:]
-            .rearrange("p g t j -> p (g t j)")
-            .bitcast(F32)
-            .rearrange("p (g t u) -> p g t u", g=PASSES, u=2)
-        )
-        for c in range(TOKEN_TILES):
-            x_words = x_sb[:, c, :].bitcast(F32)
-            for half in range(2):
-                xt = psum_t.tile([P, 2, 2, P], F32, tag="t")
-                for gi in range(2):
-                    g = 2 * half + gi
-                    for u in range(2):
-                        nc.tensor.transpose(
-                            xt[:, gi, u, :], x_words[:, 256 * g + u : 256 * (g + 1) : 2], ident_f32[:]
-                        )
-                copy = nc.vector.tensor_copy if half == 0 else nc.scalar.copy
-                copy(
-                    out=x_grouped_words[:, 2 * half : 2 * half + 2, c * P : (c + 1) * P, :],
-                    in_=xt[:].rearrange("p g u t -> p g t u"),
-                )
-
-        x_codes = keep.tile([P, PASSES, TOKENS], U32, align_bytes=64)
-        x_scales = keep.tile([P, PASSES, TOKENS], U8, align_bytes=64)
-        for g in range(PASSES):
-            nc.vector.quantize_mx(
-                out=x_codes[:, g, :].bitcast(FP8X4),
-                scales=x_scales[:, g, :],
-                in_=x_grouped[:, g, :, :].rearrange("p t j -> p (t j)"),
-            )
-
-        v_t = keep.tile([P, GROUPS, HEADS, GROUP_TOKENS], F32)
+        wv = []
         wo = []
 
-        def first_product(head):
-            w = wv[head // 4]
-            cols = slice((head % 4) * P, (head % 4 + 1) * P)
-            acc = psum_acc.tile([P, TOKENS], F32, tag="acc")
+        x_codes = {}
+        x_scales = {}
+
+        def quantise_x(half):
+            grouped = keep.tile([P, PASSES, HALF, PACK], BF16, tag="x_grouped", align_bytes=64)
+            grouped_words = (
+                grouped[:]
+                .rearrange("p g t j -> p (g t j)")
+                .bitcast(F32)
+                .rearrange("p (g t u) -> p g t u", g=PASSES, u=2)
+            )
+            for i in range(2):
+                x_words = x_sb[2 * half + i][:].bitcast(F32)
+                for g_pair in range(2):
+                    xt = psum.tile([P, 2, 2, P], F32, tag="bank")
+                    for gi in range(2):
+                        g = 2 * g_pair + gi
+                        for u in range(2):
+                            nc.tensor.transpose(
+                                xt[:, gi, u, :],
+                                x_words[:, 256 * g + u : 256 * (g + 1) : 2],
+                                ident_f32[:],
+                            )
+                    copy = nc.vector.tensor_copy if g_pair == 0 else nc.scalar.copy
+                    copy(
+                        out=grouped_words[:, 2 * g_pair : 2 * g_pair + 2, i * P : (i + 1) * P, :],
+                        in_=xt[:].rearrange("p g u t -> p g t u"),
+                    )
+            x_codes[half] = keep.tile([P, PASSES, HALF], U32, name="x_codes%d" % half, align_bytes=64)
+            x_scales[half] = keep.tile([P, PASSES, HALF], U8, name="x_scales%d" % half, align_bytes=64)
             for g in range(PASSES):
-                nc.tensor.matmul_mx(
-                    out=acc[:],
-                    lhsT=w[:, g, cols].bitcast(FP8X4),
-                    lhsT_scale=wv_planes[4 * g : P, head * P : (head + 1) * P],
-                    rhs=x_codes[:, g, :].bitcast(FP8X4),
-                    rhs_scale=x_scales[:, g, :],
-                    start=(g == 0),
-                    stop=(g == PASSES - 1),
+                nc.vector.quantize_mx(
+                    out=x_codes[half][:, g, :].bitcast(FP8X4),
+                    scales=x_scales[half][:, g, :],
+                    in_=grouped[:, g, :, :].rearrange("p t j -> p (t j)"),
                 )
+
+        v_t = keep.tile([P, GROUPS, HEADS, GROUP_TOKENS], F32)
+
+        def first_product(half, pair):
+            acc = psum.tile([P, 2, HALF], F32, tag="bank")
+            for i in range(2):
+                head = 2 * pair + i
+                for g in range(PASSES):
+                    nc.tensor.matmul_mx(
+                        out=acc[:, i, :],
+                        lhsT=wv[pair][:, g, i * P : (i + 1) * P].bitcast(FP8X4),
+                        lhsT_scale=wv_planes[4 * g : P, head * P : (head + 1) * P],
+                        rhs=x_codes[half][:, g, :].bitcast(FP8X4),
+                        rhs_scale=x_scales[half][:, g, :],
+                        start=(g == 0),
+                        stop=(g == PASSES - 1),
+                    )
+            groups = slice(half * GROUPS // 2, (half + 1) * GROUPS // 2)
             nc.scalar.copy(
-                out=v_t[:, :, head, :], in_=acc[:].rearrange("d (a t) -> d a t", t=GROUP_TOKENS)
+                out=v_t[:, groups, 2 * pair : 2 * pair + 2, :],
+                in_=acc[:].rearrange("d i (a t) -> d a i t", t=GROUP_TOKENS),
             )
 
         mixer = keep.tile([P, GROUPS, HEADS, GROUP_TOKENS], F32)
+        diff_t = keep.tile([P, GROUPS, 4, 4], F32)
 
-        def build_mixer():
+        def transpose_diff():
             diff_cols = keep.tile([P, 8, HEADS, GROUP_TOKENS], BF16)
-            nc.vector.tensor_copy(out=diff_cols[:], in_=diff_rows[:].rearrange("q c t h -> q c h t"))
-            diff_tp = psum_t.tile([P, 8, P], BF16, tag="t")
-            for c in range(8):
+            nc.scalar.copy(out=diff_cols[:], in_=diff_rows[:].rearrange("q t e h -> q e h t"))
+            diff_tp = psum.tile([P, 8, P], BF16, tag="bank")
+            for e in range(8):
                 nc.tensor.transpose(
-                    diff_tp[:, c, :],
-                    diff_cols[:, c, :, :].rearrange("q h t -> q (h t)"),
+                    diff_tp[:, e, :],
+                    diff_cols[:, e, :, :].rearrange("q h t -> q (h t)"),
                     ident_bf16[:],
                 )
-            diff_t = keep.tile([P, GROUPS, 4, 4], F32)
             nc.vector.tensor_copy(
-                out=diff_t[:],
-                in_=diff_tp[:].rearrange("k c (l hi lo) -> k (c l) lo hi", l=8, hi=4, lo=4),
+                out=diff_t[:].rearrange("k a lo (s f) -> k a lo s f", s=2),
+                in_=diff_tp[:].rearrange("k (f lo) (s a) -> k a lo s f", f=2, s=2),
             )
-            for tile_index in range(TOKEN_TILES):
-                groups = slice(tile_index * GROUPS_PER_TILE, (tile_index + 1) * GROUPS_PER_TILE)
-                shape = [P, GROUPS_PER_TILE * HEADS, GROUP_TOKENS]
-                nc.vector.tensor_tensor(
-                    out=mixer[:, groups, :, :].rearrange("k a m t -> k (a m) t"),
-                    in0=diff_t[:, groups, :, :]
-                    .rearrange("k a lo hi -> k (a lo hi)")
-                    .unsqueeze(2)
-                    .to_broadcast(shape),
-                    in1=same_token[:].unsqueeze(1).to_broadcast(shape),
-                    op=ALU.mult,
-                )
 
-        for head in range(HEADS):
-            first_product(head)
-            if head % 4 == 3:
-                wo.append(load_weight_chunk(Wo_words, head // 4))
-            if head == HEADS // 2 - 1:
-                build_mixer()
+        def build_mixer(tile_index):
+            groups = slice(tile_index * GROUPS_PER_TILE, (tile_index + 1) * GROUPS_PER_TILE)
+            shape = [P, GROUPS_PER_TILE * HEADS, GROUP_TOKENS]
+            nc.vector.tensor_tensor(
+                out=mixer[:, groups, :, :].rearrange("k a m t -> k (a m) t"),
+                in0=diff_t[:, groups, :, :]
+                .rearrange("k a lo hi -> k (a lo hi)")
+                .unsqueeze(2)
+                .to_broadcast(shape),
+                in1=same_token[:].unsqueeze(1).to_broadcast(shape),
+                op=ALU.mult,
+            )
 
         r_codes = keep.tile([P, TOKEN_TILES, PASSES * P], U32, align_bytes=64)
         r_scales = keep.tile([P, TOKEN_TILES, PASSES * P], U8, align_bytes=64)
@@ -216,7 +216,7 @@ def tile_differentialattention_pb_kernel(
         r_grouped = {}
 
         def transpose_v(bank):
-            v_tp = psum_t.tile([P, GROUPS_PER_BANK, HEAD_DIM], F32, tag="t")
+            v_tp = psum.tile([P, GROUPS_PER_BANK, HEAD_DIM], F32, tag="bank")
             for i in range(GROUPS_PER_BANK):
                 nc.tensor.transpose(
                     v_tp[:, i, :],
@@ -230,7 +230,7 @@ def tile_differentialattention_pb_kernel(
         def mix_and_norm(bank):
             tile_index, bank_in_tile = divmod(bank, BANKS_PER_TILE)
             v_g = v_groups[bank]
-            mixed = psum_mix.tile([P, GROUPS_PER_BANK, HEAD_DIM], F32, tag="mix")
+            mixed = psum.tile([P, GROUPS_PER_BANK, HEAD_DIM], F32, tag="bank")
             for i in range(GROUPS_PER_BANK):
                 nc.tensor.matmul(
                     out=mixed[:, i, :],
@@ -240,7 +240,7 @@ def tile_differentialattention_pb_kernel(
                     stop=True,
                 )
             squares = work.tile([P, GROUPS_PER_BANK, HEAD_DIM], BF16, tag="squares")
-            sum_sq = stats.tile([P, GROUPS_PER_BANK], F32, tag="sum_sq")
+            sum_sq = work.tile([P, GROUPS_PER_BANK], F32, tag="sum_sq")
             for i in range(GROUPS_PER_BANK):
                 nc.scalar.activation(
                     out=squares[:, i, :],
@@ -248,7 +248,7 @@ def tile_differentialattention_pb_kernel(
                     func=ACT.Square,
                     accum_out=sum_sq[:, i : i + 1],
                 )
-            root = stats.tile([P, GROUPS_PER_BANK], F32, tag="root")
+            root = work.tile([P, GROUPS_PER_BANK], F32, tag="root")
             nc.scalar.activation(
                 out=root[:],
                 in_=sum_sq[:],
@@ -256,7 +256,7 @@ def tile_differentialattention_pb_kernel(
                 scale=1.0 / (HEAD_DIM * KEEP * KEEP),
                 bias=EPS / (KEEP * KEEP),
             )
-            gain = stats.tile([P, GROUPS_PER_BANK], F32, tag="gain")
+            gain = work.tile([P, GROUPS_PER_BANK], F32, tag="gain")
             nc.vector.reciprocal(out=gain[:], in_=root[:])
             r_rows = work.tile([P, GROUPS_PER_BANK, HEAD_DIM], BF16, tag="r_rows", align_bytes=64)
             nc.vector.tensor_tensor(
@@ -265,7 +265,7 @@ def tile_differentialattention_pb_kernel(
                 in1=gain[:].unsqueeze(2).to_broadcast([P, GROUPS_PER_BANK, HEAD_DIM]),
                 op=ALU.mult,
             )
-            r_cols = work.tile([P, CHUNK], BF16, tag="r_cols", align_bytes=64)
+            r_cols = work.tile([P, BANK], BF16, tag="r_cols", align_bytes=64)
             nc.vector.transpose(out=r_cols[:], in_=r_rows[:].rearrange("m i c -> m (i c)"))
             if bank_in_tile == 0:
                 r_grouped[tile_index] = work.tile(
@@ -290,29 +290,68 @@ def tile_differentialattention_pb_kernel(
                     in_=r_grouped[tile_index][:].rearrange("p g a t j -> p (g a t j)"),
                 )
 
-        def second_product(tile_index):
-            for chunk in range(N_CHUNKS):
-                cols = slice(chunk * CHUNK, (chunk + 1) * CHUNK)
-                acc = psum_acc.tile([P, CHUNK], F32, tag="acc")
-                for g in range(PASSES):
-                    nc.tensor.matmul_mx(
-                        out=acc[:],
-                        lhsT=r_codes[:, tile_index, g * P : (g + 1) * P].bitcast(FP8X4),
-                        lhsT_scale=r_scales[:, tile_index, g * P : (g + 1) * P],
-                        rhs=wo[chunk][:, g, :].bitcast(FP8X4),
-                        rhs_scale=wo_planes[4 * g : P, cols],
-                        start=(g == 0),
-                        stop=(g == PASSES - 1),
-                    )
-                result = work.tile([P, CHUNK], F32, tag="result")
-                nc.vector.tensor_tensor(out=result[:], in0=acc[:], in1=bias[:, cols], op=ALU.add)
-                nc.sync.dma_start(out=out_view[tile_index][:, :, cols], in_=result[:])
+        def second_product(tile_index, chunk):
+            cols = slice(chunk * BANK, (chunk + 1) * BANK)
+            acc = psum.tile([P, BANK], F32, tag="bank")
+            for g in range(PASSES):
+                nc.tensor.matmul_mx(
+                    out=acc[:],
+                    lhsT=r_codes[:, tile_index, g * P : (g + 1) * P].bitcast(FP8X4),
+                    lhsT_scale=r_scales[:, tile_index, g * P : (g + 1) * P],
+                    rhs=wo[chunk][:, g, :].bitcast(FP8X4),
+                    rhs_scale=wo_planes[4 * g : P, cols],
+                    start=(g == 0),
+                    stop=(g == PASSES - 1),
+                )
+            result = work.tile([P, BANK], F32, tag="result")
+            nc.vector.tensor_tensor(out=result[:], in0=acc[:], in1=bias[:, cols], op=ALU.add)
+            nc.sync.dma_start(
+                out=out_rows[tile_index * P : (tile_index + 1) * P, cols], in_=result[:]
+            )
+
+        load_x(0)
+        load_x(1)
+        load_diff()
+        load_scale_planes(wv_planes, Wv_scales)
+        wv.extend([load_wv(pair) for pair in range(HEAD_PAIRS // 2)])
+        quantise_x(0)
+        load_x(2)
+        load_x(3)
+        wv.extend([load_wv(pair) for pair in range(HEAD_PAIRS // 2, HEAD_PAIRS)])
+        nc.sync.dma_start(out=bias[:], in_=bo.partition_broadcast(P))
+        load_scale_planes(wo_planes, Wo_scales)
+        wo.extend(
+            [
+                load_weight_columns(Wo_words, chunk * BANK, BANK, "wo%d" % chunk)
+                for chunk in range(N_CHUNKS)
+            ]
+        )
+        transpose_diff()
+        for pair in range(HEAD_PAIRS // 2):
+            first_product(0, pair)
+        build_mixer(0)
+        quantise_x(1)
+        build_mixer(1)
+        for pair in range(HEAD_PAIRS // 2, HEAD_PAIRS):
+            first_product(0, pair)
+        build_mixer(2)
+        build_mixer(3)
 
         transpose_v(0)
-        for bank in range(BANKS):
-            if bank + 1 < BANKS:
-                transpose_v(bank + 1)
-            mix_and_norm(bank)
-            if bank % BANKS_PER_TILE == BANKS_PER_TILE - 1 and bank >= 2 * BANKS_PER_TILE - 1:
-                second_product(bank // BANKS_PER_TILE - 1)
-        second_product(TOKEN_TILES - 1)
+        transpose_v(1)
+        for step in range(STEPS):
+            if step < STEPS // 2:
+                first_product(1, 2 * step)
+                first_product(1, 2 * step + 1)
+            else:
+                tile_index, chunk_pair = divmod(step - STEPS // 2, 2)
+                second_product(tile_index, 2 * chunk_pair)
+                second_product(tile_index, 2 * chunk_pair + 1)
+            mix_and_norm(2 * step)
+            mix_and_norm(2 * step + 1)
+            if step + 1 < STEPS:
+                transpose_v(2 * step + 2)
+                transpose_v(2 * step + 3)
+        for tile_index in range(TOKEN_TILES // 2, TOKEN_TILES):
+            for chunk in range(N_CHUNKS):
+                second_product(tile_index, chunk)

@@ -66,6 +66,12 @@ def tile_differentialattention_pb_kernel(
         ident_bf16 = const.tile([P, P], BF16)
         make_identity(nc, ident_bf16[:])
 
+        by_word = const.tile([P, P], F32)
+        nc.vector.tensor_copy(
+            out=by_word[:].rearrange("p (j q) -> p j q", j=PACK),
+            in_=ident_f32[:].rearrange("p (q j) -> p j q", j=PACK),
+        )
+
         one = const.tile([P, 1], F32)
         nc.vector.memset(one[:], 1.0)
         one_root = const.tile([P, 1], F32)
@@ -174,7 +180,8 @@ def tile_differentialattention_pb_kernel(
                         stop=(g == PASSES - 1),
                     )
             groups = slice(half * GROUPS // 2, (half + 1) * GROUPS // 2)
-            nc.scalar.copy(
+            copy = nc.scalar.copy if half == 0 else nc.vector.tensor_copy
+            copy(
                 out=v_t[:, groups, 2 * pair : 2 * pair + 2, :],
                 in_=acc[:].rearrange("d i (a t) -> d a i t", t=GROUP_TOKENS),
             )
@@ -184,7 +191,14 @@ def tile_differentialattention_pb_kernel(
 
         def transpose_diff():
             diff_cols = keep.tile([P, 8, HEADS, GROUP_TOKENS], BF16)
-            nc.scalar.copy(out=diff_cols[:], in_=diff_rows[:].rearrange("q t e h -> q e h t"))
+            nc.gpsimd.tensor_scalar(
+                out=diff_cols[:],
+                in0=diff_rows[:].rearrange("q t e h -> q e h t"),
+                scalar1=1.0,
+                scalar2=0.0,
+                op0=ALU.mult,
+                op1=ALU.add,
+            )
             diff_tp = psum.tile([P, 8, P], BF16, tag="bank")
             for e in range(8):
                 nc.tensor.transpose(
@@ -213,6 +227,7 @@ def tile_differentialattention_pb_kernel(
         r_codes = keep.tile([P, TOKEN_TILES, PASSES * P], U32, align_bytes=64)
         r_scales = keep.tile([P, TOKEN_TILES, PASSES * P], U8, align_bytes=64)
         v_groups = {}
+        r_columns = {}
         r_grouped = {}
 
         def transpose_v(bank):
@@ -221,21 +236,20 @@ def tile_differentialattention_pb_kernel(
                 nc.tensor.transpose(
                     v_tp[:, i, :],
                     v_t[:, bank * GROUPS_PER_BANK + i, :, :].rearrange("d h t -> d (h t)"),
-                    ident_f32[:],
+                    by_word[:],
                 )
-            v_g = work.tile([P, GROUPS_PER_BANK, PACK, 32], F32, tag="v_g")
-            nc.scalar.copy(out=v_g[:], in_=v_tp[:].rearrange("k i (q j) -> k i j q", j=PACK))
+            v_g = work.tile([P, GROUPS_PER_BANK, HEAD_DIM], F32, tag="v_g")
+            nc.scalar.copy(out=v_g[:], in_=v_tp[:])
             v_groups[bank] = v_g
 
         def mix_and_norm(bank):
-            tile_index, bank_in_tile = divmod(bank, BANKS_PER_TILE)
             v_g = v_groups[bank]
             mixed = psum.tile([P, GROUPS_PER_BANK, HEAD_DIM], F32, tag="bank")
             for i in range(GROUPS_PER_BANK):
                 nc.tensor.matmul(
                     out=mixed[:, i, :],
                     lhsT=mixer[:, bank * GROUPS_PER_BANK + i, :, :].rearrange("k m t -> k (m t)"),
-                    rhs=v_g[:, i, :, :].rearrange("k j q -> k (j q)"),
+                    rhs=v_g[:, i, :],
                     start=True,
                     stop=True,
                 )
@@ -267,6 +281,10 @@ def tile_differentialattention_pb_kernel(
             )
             r_cols = work.tile([P, BANK], BF16, tag="r_cols", align_bytes=64)
             nc.vector.transpose(out=r_cols[:], in_=r_rows[:].rearrange("m i c -> m (i c)"))
+            r_columns[bank] = r_cols
+
+        def group_and_quantise(bank):
+            tile_index, bank_in_tile = divmod(bank, BANKS_PER_TILE)
             if bank_in_tile == 0:
                 r_grouped[tile_index] = work.tile(
                     [P, PASSES, GROUPS_PER_TILE, GROUP_TOKENS, PACK],
@@ -277,12 +295,14 @@ def tile_differentialattention_pb_kernel(
                     align_bytes=64,
                 )
             first = bank_in_tile * GROUPS_PER_BANK
-            nc.vector.tensor_copy(
-                out=r_grouped[tile_index][:, :, first : first + GROUPS_PER_BANK, :, :],
-                in_=r_cols[:].rearrange(
-                    "p (a j hi t) -> p hi a t j", a=GROUPS_PER_BANK, j=PACK, hi=PASSES
-                ),
+            by_pass = r_columns[bank][:].rearrange(
+                "p (a j hi t) -> p hi a t j", a=GROUPS_PER_BANK, j=PACK, hi=PASSES
             )
+            for g in range(PASSES):
+                nc.scalar.copy(
+                    out=r_grouped[tile_index][:, g, first : first + GROUPS_PER_BANK, :, :],
+                    in_=by_pass[:, g, :, :, :],
+                )
             if bank_in_tile == BANKS_PER_TILE - 1:
                 nc.vector.quantize_mx(
                     out=r_codes[:, tile_index, :].bitcast(FP8X4),
@@ -337,12 +357,13 @@ def tile_differentialattention_pb_kernel(
         build_mixer(2)
         build_mixer(3)
 
+        first_product(1, 0)
         transpose_v(0)
         transpose_v(1)
         for step in range(STEPS):
             if step < STEPS // 2:
-                first_product(1, 2 * step)
-                first_product(1, 2 * step + 1)
+                for pair in range(2 * step + 1, min(2 * step + 3, HEAD_PAIRS)):
+                    first_product(1, pair)
             else:
                 tile_index, chunk_pair = divmod(step - STEPS // 2, 2)
                 second_product(tile_index, 2 * chunk_pair)
@@ -352,6 +373,8 @@ def tile_differentialattention_pb_kernel(
             if step + 1 < STEPS:
                 transpose_v(2 * step + 2)
                 transpose_v(2 * step + 3)
+            group_and_quantise(2 * step)
+            group_and_quantise(2 * step + 1)
         for tile_index in range(TOKEN_TILES // 2, TOKEN_TILES):
             for chunk in range(N_CHUNKS):
                 second_product(tile_index, chunk)

@@ -31,9 +31,9 @@ GROUP_TOKENS = 8
 GROUPS = TOKENS // GROUP_TOKENS
 GROUPS_PER_BANK = BANK // HEAD_DIM
 MIX_BANKS = GROUPS // GROUPS_PER_BANK
-BANKS_PER_TILE = MIX_BANKS // TOKEN_TILES
 GROUPS_PER_TILE = GROUPS // TOKEN_TILES
 STEPS = MIX_BANKS // 2
+STEPS_PER_TILE = STEPS // TOKEN_TILES
 
 L0 = 0.8 - 0.6 * math.exp(-0.3 * 12)
 KEEP = 1.0 - L0
@@ -52,7 +52,7 @@ def tile_differentialattention_pb_kernel(
     with ExitStack() as ctx:
         const = ctx.enter_context(tc.tile_pool(name="const", bufs=1))
         keep = ctx.enter_context(tc.tile_pool(name="keep", bufs=1))
-        work = ctx.enter_context(tc.tile_pool(name="work", bufs=4))
+        work = ctx.enter_context(tc.tile_pool(name="work", bufs=3))
         psum = ctx.enter_context(tc.psum_pool(name="psum", bufs=PSUM_BANKS))
         ctx.enter_context(tc.manual_schedule())
 
@@ -65,12 +65,6 @@ def tile_differentialattention_pb_kernel(
         make_identity(nc, ident_f32[:])
         ident_bf16 = const.tile([P, P], BF16)
         make_identity(nc, ident_bf16[:])
-
-        by_word = const.tile([P, P], F32)
-        nc.vector.tensor_copy(
-            out=by_word[:].rearrange("p (j q) -> p j q", j=PACK),
-            in_=ident_f32[:].rearrange("p (q j) -> p j q", j=PACK),
-        )
 
         one = const.tile([P, 1], F32)
         nc.vector.memset(one[:], 1.0)
@@ -156,12 +150,11 @@ def tile_differentialattention_pb_kernel(
                     )
             x_codes[half] = keep.tile([P, PASSES, HALF], U32, name="x_codes%d" % half, align_bytes=64)
             x_scales[half] = keep.tile([P, PASSES, HALF], U8, name="x_scales%d" % half, align_bytes=64)
-            for g in range(PASSES):
-                nc.vector.quantize_mx(
-                    out=x_codes[half][:, g, :].bitcast(FP8X4),
-                    scales=x_scales[half][:, g, :],
-                    in_=grouped[:, g, :, :].rearrange("p t j -> p (t j)"),
-                )
+            nc.vector.quantize_mx(
+                out=x_codes[half][:].rearrange("p g t -> p (g t)").bitcast(FP8X4),
+                scales=x_scales[half][:].rearrange("p g t -> p (g t)"),
+                in_=grouped[:].rearrange("p g t j -> p (g t j)"),
+            )
 
         v_t = keep.tile([P, GROUPS, HEADS, GROUP_TOKENS], F32)
 
@@ -180,7 +173,7 @@ def tile_differentialattention_pb_kernel(
                         stop=(g == PASSES - 1),
                     )
             groups = slice(half * GROUPS // 2, (half + 1) * GROUPS // 2)
-            copy = nc.scalar.copy if half == 0 else nc.vector.tensor_copy
+            copy = nc.vector.tensor_copy if half == 1 and pair % 2 == 1 else nc.scalar.copy
             copy(
                 out=v_t[:, groups, 2 * pair : 2 * pair + 2, :],
                 in_=acc[:].rearrange("d i (a t) -> d a i t", t=GROUP_TOKENS),
@@ -191,14 +184,7 @@ def tile_differentialattention_pb_kernel(
 
         def transpose_diff():
             diff_cols = keep.tile([P, 8, HEADS, GROUP_TOKENS], BF16)
-            nc.gpsimd.tensor_scalar(
-                out=diff_cols[:],
-                in0=diff_rows[:].rearrange("q t e h -> q e h t"),
-                scalar1=1.0,
-                scalar2=0.0,
-                op0=ALU.mult,
-                op1=ALU.add,
-            )
+            nc.scalar.copy(out=diff_cols[:], in_=diff_rows[:].rearrange("q t e h -> q e h t"))
             diff_tp = psum.tile([P, 8, P], BF16, tag="bank")
             for e in range(8):
                 nc.tensor.transpose(
@@ -227,7 +213,6 @@ def tile_differentialattention_pb_kernel(
         r_codes = keep.tile([P, TOKEN_TILES, PASSES * P], U32, align_bytes=64)
         r_scales = keep.tile([P, TOKEN_TILES, PASSES * P], U8, align_bytes=64)
         v_groups = {}
-        r_columns = {}
         r_grouped = {}
 
         def transpose_v(bank):
@@ -236,33 +221,36 @@ def tile_differentialattention_pb_kernel(
                 nc.tensor.transpose(
                     v_tp[:, i, :],
                     v_t[:, bank * GROUPS_PER_BANK + i, :, :].rearrange("d h t -> d (h t)"),
-                    by_word[:],
+                    ident_f32[:],
                 )
-            v_g = work.tile([P, GROUPS_PER_BANK, HEAD_DIM], F32, tag="v_g")
-            nc.scalar.copy(out=v_g[:], in_=v_tp[:])
+            v_g = work.tile([P, GROUPS_PER_BANK, PACK, 32], F32, tag="v_g")
+            nc.scalar.copy(out=v_g[:], in_=v_tp[:].rearrange("k i (q j) -> k i j q", j=PACK))
             v_groups[bank] = v_g
 
-        def mix_and_norm(bank):
-            v_g = v_groups[bank]
-            mixed = psum.tile([P, GROUPS_PER_BANK, HEAD_DIM], F32, tag="bank")
-            for i in range(GROUPS_PER_BANK):
-                nc.tensor.matmul(
-                    out=mixed[:, i, :],
-                    lhsT=mixer[:, bank * GROUPS_PER_BANK + i, :, :].rearrange("k m t -> k (m t)"),
-                    rhs=v_g[:, i, :],
-                    start=True,
-                    stop=True,
-                )
-            squares = work.tile([P, GROUPS_PER_BANK, HEAD_DIM], BF16, tag="squares")
-            sum_sq = work.tile([P, GROUPS_PER_BANK], F32, tag="sum_sq")
-            for i in range(GROUPS_PER_BANK):
-                nc.scalar.activation(
-                    out=squares[:, i, :],
-                    in_=mixed[:, i, :],
-                    func=ACT.Square,
-                    accum_out=sum_sq[:, i : i + 1],
-                )
-            root = work.tile([P, GROUPS_PER_BANK], F32, tag="root")
+        def mix_and_norm(step):
+            tile_index, step_in_tile = divmod(step, STEPS_PER_TILE)
+            mixed = []
+            for bank in (2 * step, 2 * step + 1):
+                mixed.append(psum.tile([P, GROUPS_PER_BANK, HEAD_DIM], F32, name="mixed", tag="bank"))
+                for i in range(GROUPS_PER_BANK):
+                    nc.tensor.matmul(
+                        out=mixed[-1][:, i, :],
+                        lhsT=mixer[:, bank * GROUPS_PER_BANK + i, :, :].rearrange("k m t -> k (m t)"),
+                        rhs=v_groups[bank][:, i, :, :].rearrange("k j q -> k (j q)"),
+                        start=True,
+                        stop=True,
+                    )
+            squares = work.tile([P, 2, GROUPS_PER_BANK, HEAD_DIM], BF16, tag="squares")
+            sum_sq = work.tile([P, 2, GROUPS_PER_BANK], F32, tag="sum_sq")
+            for b in range(2):
+                for i in range(GROUPS_PER_BANK):
+                    nc.scalar.activation(
+                        out=squares[:, b, i, :],
+                        in_=mixed[b][:, i, :],
+                        func=ACT.Square,
+                        accum_out=sum_sq[:, b, i : i + 1],
+                    )
+            root = work.tile([P, 2, GROUPS_PER_BANK], F32, tag="root")
             nc.scalar.activation(
                 out=root[:],
                 in_=sum_sq[:],
@@ -270,22 +258,19 @@ def tile_differentialattention_pb_kernel(
                 scale=1.0 / (HEAD_DIM * KEEP * KEEP),
                 bias=EPS / (KEEP * KEEP),
             )
-            gain = work.tile([P, GROUPS_PER_BANK], F32, tag="gain")
+            gain = work.tile([P, 2, GROUPS_PER_BANK], F32, tag="gain")
             nc.vector.reciprocal(out=gain[:], in_=root[:])
-            r_rows = work.tile([P, GROUPS_PER_BANK, HEAD_DIM], BF16, tag="r_rows", align_bytes=64)
-            nc.vector.tensor_tensor(
-                out=r_rows[:],
-                in0=mixed[:],
-                in1=gain[:].unsqueeze(2).to_broadcast([P, GROUPS_PER_BANK, HEAD_DIM]),
-                op=ALU.mult,
-            )
-            r_cols = work.tile([P, BANK], BF16, tag="r_cols", align_bytes=64)
-            nc.vector.transpose(out=r_cols[:], in_=r_rows[:].rearrange("m i c -> m (i c)"))
-            r_columns[bank] = r_cols
-
-        def group_and_quantise(bank):
-            tile_index, bank_in_tile = divmod(bank, BANKS_PER_TILE)
-            if bank_in_tile == 0:
+            r_rows = work.tile([P, 2, GROUPS_PER_BANK, HEAD_DIM], BF16, tag="r_rows", align_bytes=64)
+            for b in range(2):
+                nc.vector.tensor_tensor(
+                    out=r_rows[:, b, :, :],
+                    in0=mixed[b][:],
+                    in1=gain[:, b, :].unsqueeze(2).to_broadcast([P, GROUPS_PER_BANK, HEAD_DIM]),
+                    op=ALU.mult,
+                )
+            r_cols = work.tile([P, 2 * BANK], BF16, tag="r_cols", align_bytes=64)
+            nc.vector.transpose(out=r_cols[:], in_=r_rows[:].rearrange("m b i c -> m (b i c)"))
+            if step_in_tile == 0:
                 r_grouped[tile_index] = work.tile(
                     [P, PASSES, GROUPS_PER_TILE, GROUP_TOKENS, PACK],
                     BF16,
@@ -294,16 +279,14 @@ def tile_differentialattention_pb_kernel(
                     bufs=2,
                     align_bytes=64,
                 )
-            first = bank_in_tile * GROUPS_PER_BANK
-            by_pass = r_columns[bank][:].rearrange(
-                "p (a j hi t) -> p hi a t j", a=GROUPS_PER_BANK, j=PACK, hi=PASSES
+            first = step_in_tile * 2 * GROUPS_PER_BANK
+            nc.vector.tensor_copy(
+                out=r_grouped[tile_index][:, :, first : first + 2 * GROUPS_PER_BANK, :, :],
+                in_=r_cols[:].rearrange(
+                    "p (a j hi t) -> p hi a t j", a=2 * GROUPS_PER_BANK, j=PACK, hi=PASSES
+                ),
             )
-            for g in range(PASSES):
-                nc.scalar.copy(
-                    out=r_grouped[tile_index][:, g, first : first + GROUPS_PER_BANK, :, :],
-                    in_=by_pass[:, g, :, :, :],
-                )
-            if bank_in_tile == BANKS_PER_TILE - 1:
+            if step_in_tile == STEPS_PER_TILE - 1:
                 nc.vector.quantize_mx(
                     out=r_codes[:, tile_index, :].bitcast(FP8X4),
                     scales=r_scales[:, tile_index, :],
@@ -323,7 +306,7 @@ def tile_differentialattention_pb_kernel(
                     start=(g == 0),
                     stop=(g == PASSES - 1),
                 )
-            result = work.tile([P, BANK], F32, tag="result")
+            result = work.tile([P, BANK], F32, tag="result", bufs=4)
             nc.vector.tensor_tensor(out=result[:], in0=acc[:], in1=bias[:, cols], op=ALU.add)
             nc.sync.dma_start(
                 out=out_rows[tile_index * P : (tile_index + 1) * P, cols], in_=result[:]
@@ -357,24 +340,20 @@ def tile_differentialattention_pb_kernel(
         build_mixer(2)
         build_mixer(3)
 
-        first_product(1, 0)
         transpose_v(0)
         transpose_v(1)
         for step in range(STEPS):
             if step < STEPS // 2:
-                for pair in range(2 * step + 1, min(2 * step + 3, HEAD_PAIRS)):
-                    first_product(1, pair)
+                first_product(1, 2 * step)
+                first_product(1, 2 * step + 1)
             else:
                 tile_index, chunk_pair = divmod(step - STEPS // 2, 2)
                 second_product(tile_index, 2 * chunk_pair)
                 second_product(tile_index, 2 * chunk_pair + 1)
-            mix_and_norm(2 * step)
-            mix_and_norm(2 * step + 1)
+            mix_and_norm(step)
             if step + 1 < STEPS:
                 transpose_v(2 * step + 2)
                 transpose_v(2 * step + 3)
-            group_and_quantise(2 * step)
-            group_and_quantise(2 * step + 1)
         for tile_index in range(TOKEN_TILES // 2, TOKEN_TILES):
             for chunk in range(N_CHUNKS):
                 second_product(tile_index, chunk)

@@ -223,8 +223,10 @@ def tile_differentialattention_pb_kernel(
                     v_t[:, bank * GROUPS_PER_BANK + i, :, :].rearrange("d h t -> d (h t)"),
                     ident_f32[:],
                 )
-            v_g = work.tile([P, GROUPS_PER_BANK, PACK, 32], F32, tag="v_g")
-            nc.scalar.copy(out=v_g[:], in_=v_tp[:].rearrange("k i (q j) -> k i j q", j=PACK))
+            v_g = work.tile([P, GROUPS_PER_BANK, 2, 32, 2], F32, tag="v_g")
+            nc.scalar.copy(
+                out=v_g[:], in_=v_tp[:].rearrange("k i (q jp j2) -> k i jp q j2", jp=2, j2=2)
+            )
             v_groups[bank] = v_g
 
         def mix_and_norm(step):
@@ -236,7 +238,7 @@ def tile_differentialattention_pb_kernel(
                     nc.tensor.matmul(
                         out=mixed[-1][:, i, :],
                         lhsT=mixer[:, bank * GROUPS_PER_BANK + i, :, :].rearrange("k m t -> k (m t)"),
-                        rhs=v_groups[bank][:, i, :, :].rearrange("k j q -> k (j q)"),
+                        rhs=v_groups[bank][:, i, :, :, :].rearrange("k jp q j2 -> k (jp q j2)"),
                         start=True,
                         stop=True,
                     )
@@ -269,7 +271,10 @@ def tile_differentialattention_pb_kernel(
                     op=ALU.mult,
                 )
             r_cols = work.tile([P, 2 * BANK], BF16, tag="r_cols", align_bytes=64)
-            nc.vector.transpose(out=r_cols[:], in_=r_rows[:].rearrange("m b i c -> m (b i c)"))
+            nc.vector.transpose(
+                out=r_cols[:].bitcast(F32),
+                in_=r_rows[:].rearrange("m b i c -> m (b i c)").bitcast(F32),
+            )
             if step_in_tile == 0:
                 r_grouped[tile_index] = work.tile(
                     [P, PASSES, GROUPS_PER_TILE, GROUP_TOKENS, PACK],
@@ -280,11 +285,17 @@ def tile_differentialattention_pb_kernel(
                     align_bytes=64,
                 )
             first = step_in_tile * 2 * GROUPS_PER_BANK
+            grouped_words = (
+                r_grouped[tile_index][:]
+                .rearrange("p g a t j -> p (g a t j)")
+                .bitcast(F32)
+                .rearrange("p (g a t jp) -> p g a t jp", g=PASSES, a=GROUPS_PER_TILE, jp=2)
+            )
             nc.vector.tensor_copy(
-                out=r_grouped[tile_index][:, :, first : first + 2 * GROUPS_PER_BANK, :, :],
-                in_=r_cols[:].rearrange(
-                    "p (a j hi t) -> p hi a t j", a=2 * GROUPS_PER_BANK, j=PACK, hi=PASSES
-                ),
+                out=grouped_words[:, :, first : first + 2 * GROUPS_PER_BANK, :, :],
+                in_=r_cols[:]
+                .bitcast(F32)
+                .rearrange("p (a jp hi t) -> p hi a t jp", a=2 * GROUPS_PER_BANK, jp=2, hi=PASSES),
             )
             if step_in_tile == STEPS_PER_TILE - 1:
                 nc.vector.quantize_mx(

@@ -82,7 +82,7 @@ def tile_differentialattention_pb_kernel(
         x_sb = {}
 
         def load_x(tile_index):
-            x_sb[tile_index] = keep.tile([P, WIDTH], BF16, name="x_sb", tag="x_sb", bufs=2)
+            x_sb[tile_index] = keep.tile([P, WIDTH], BF16, name="x_sb", tag="x_sb", bufs=TOKEN_TILES)
             nc.sync.dma_start(
                 out=x_sb[tile_index][:], in_=x_rows[tile_index * P : (tile_index + 1) * P, :]
             )
@@ -124,7 +124,7 @@ def tile_differentialattention_pb_kernel(
         x_scales = {}
 
         def quantise_x(half):
-            grouped = keep.tile([P, PASSES, HALF, PACK], BF16, tag="x_grouped", align_bytes=64)
+            grouped = keep.tile([P, PASSES, HALF, PACK], BF16, tag="x_grouped", bufs=2, align_bytes=64)
             grouped_words = (
                 grouped[:]
                 .rearrange("p g t j -> p (g t j)")
@@ -182,9 +182,12 @@ def tile_differentialattention_pb_kernel(
         mixer = keep.tile([P, GROUPS, HEADS, GROUP_TOKENS], F32)
         diff_t = keep.tile([P, GROUPS, 4, 4], F32)
 
+        diff_cols = keep.tile([P, 8, HEADS, GROUP_TOKENS], BF16)
+
+        def order_diff():
+            nc.vector.tensor_copy(out=diff_cols[:], in_=diff_rows[:].rearrange("q t e h -> q e h t"))
+
         def transpose_diff():
-            diff_cols = keep.tile([P, 8, HEADS, GROUP_TOKENS], BF16)
-            nc.scalar.copy(out=diff_cols[:], in_=diff_rows[:].rearrange("q t e h -> q e h t"))
             diff_tp = psum.tile([P, 8, P], BF16, tag="bank")
             for e in range(8):
                 nc.tensor.transpose(
@@ -323,15 +326,12 @@ def tile_differentialattention_pb_kernel(
                 out=out_rows[tile_index * P : (tile_index + 1) * P, cols], in_=result[:]
             )
 
-        load_x(0)
-        load_x(1)
-        load_diff()
+        for tile_index in range(TOKEN_TILES):
+            load_x(tile_index)
         load_scale_planes(wv_planes, Wv_scales)
-        wv.extend([load_wv(pair) for pair in range(HEAD_PAIRS // 2)])
-        quantise_x(0)
-        load_x(2)
-        load_x(3)
-        wv.extend([load_wv(pair) for pair in range(HEAD_PAIRS // 2, HEAD_PAIRS)])
+        wv.extend([load_wv(pair) for pair in range(2)])
+        load_diff()
+        wv.extend([load_wv(pair) for pair in range(2, HEAD_PAIRS)])
         nc.sync.dma_start(out=bias[:], in_=bo.partition_broadcast(P))
         load_scale_planes(wo_planes, Wo_scales)
         wo.extend(
@@ -340,23 +340,25 @@ def tile_differentialattention_pb_kernel(
                 for chunk in range(N_CHUNKS)
             ]
         )
-        transpose_diff()
-        for pair in range(HEAD_PAIRS // 2):
-            first_product(0, pair)
-        build_mixer(0)
+        quantise_x(0)
         quantise_x(1)
-        build_mixer(1)
-        for pair in range(HEAD_PAIRS // 2, HEAD_PAIRS):
+        order_diff()
+        for pair in range(3):
             first_product(0, pair)
-        build_mixer(2)
-        build_mixer(3)
+        transpose_diff()
+        for pair in range(3, HEAD_PAIRS):
+            first_product(0, pair)
+        for tile_index in range(TOKEN_TILES):
+            build_mixer(tile_index)
 
+        first_product(1, 0)
         transpose_v(0)
         transpose_v(1)
         for step in range(STEPS):
             if step < STEPS // 2:
-                first_product(1, 2 * step)
-                first_product(1, 2 * step + 1)
+                for pair in (2 * step + 1, 2 * step + 2):
+                    if pair < HEAD_PAIRS:
+                        first_product(1, pair)
             else:
                 tile_index, chunk_pair = divmod(step - STEPS // 2, 2)
                 second_product(tile_index, 2 * chunk_pair)

@@ -173,7 +173,7 @@ def tile_differentialattention_pb_kernel(
                         stop=(g == PASSES - 1),
                     )
             groups = slice(half * GROUPS // 2, (half + 1) * GROUPS // 2)
-            copy = nc.vector.tensor_copy if half == 1 and pair % 2 == 1 else nc.scalar.copy
+            copy = nc.vector.tensor_copy if half == 1 else nc.scalar.copy
             copy(
                 out=v_t[:, groups, 2 * pair : 2 * pair + 2, :],
                 in_=acc[:].rearrange("d i (a t) -> d a i t", t=GROUP_TOKENS),
@@ -226,13 +226,13 @@ def tile_differentialattention_pb_kernel(
                     v_t[:, bank * GROUPS_PER_BANK + i, :, :].rearrange("d h t -> d (h t)"),
                     ident_f32[:],
                 )
-            v_g = work.tile([P, GROUPS_PER_BANK, 2, 32, 2], F32, tag="v_g")
+            v_g = work.tile([P, GROUPS_PER_BANK, 2, 32, 2], F32, tag="v_g", bufs=6)
             nc.scalar.copy(
                 out=v_g[:], in_=v_tp[:].rearrange("k i (q jp j2) -> k i jp q j2", jp=2, j2=2)
             )
             v_groups[bank] = v_g
 
-        def mix_and_norm(step):
+        def mix_and_norm(step, behind_mix=()):
             tile_index, step_in_tile = divmod(step, STEPS_PER_TILE)
             mixed = []
             for bank in (2 * step, 2 * step + 1):
@@ -245,7 +245,9 @@ def tile_differentialattention_pb_kernel(
                         start=True,
                         stop=True,
                     )
-            squares = work.tile([P, 2, GROUPS_PER_BANK, HEAD_DIM], BF16, tag="squares")
+            for out_tile, chunk in behind_mix:
+                second_product(out_tile, chunk)
+            squares = work.tile([P, 2, GROUPS_PER_BANK, HEAD_DIM], BF16, tag="squares", bufs=1)
             sum_sq = work.tile([P, 2, GROUPS_PER_BANK], F32, tag="sum_sq")
             for b in range(2):
                 for i in range(GROUPS_PER_BANK):
@@ -265,7 +267,7 @@ def tile_differentialattention_pb_kernel(
             )
             gain = work.tile([P, 2, GROUPS_PER_BANK], F32, tag="gain")
             nc.vector.reciprocal(out=gain[:], in_=root[:])
-            r_rows = work.tile([P, 2, GROUPS_PER_BANK, HEAD_DIM], BF16, tag="r_rows", align_bytes=64)
+            r_rows = work.tile([P, 2, GROUPS_PER_BANK, HEAD_DIM], BF16, tag="r_rows", bufs=2, align_bytes=64)
             for b in range(2):
                 nc.vector.tensor_tensor(
                     out=r_rows[:, b, :, :],
@@ -343,30 +345,33 @@ def tile_differentialattention_pb_kernel(
         quantise_x(0)
         quantise_x(1)
         order_diff()
-        for pair in range(3):
+        for pair in range(2):
             first_product(0, pair)
+        for pair in range(2):
+            first_product(1, pair)
+        first_product(0, 2)
         transpose_diff()
-        for pair in range(3, HEAD_PAIRS):
+        first_product(1, 2)
+        for pair in range(3, HEAD_PAIRS - 2):
             first_product(0, pair)
-        for tile_index in range(TOKEN_TILES):
-            build_mixer(tile_index)
+            first_product(1, pair)
+            build_mixer(pair - 3)
+        first_product(0, HEAD_PAIRS - 2)
+        first_product(0, HEAD_PAIRS - 1)
+        build_mixer(3)
+        first_product(1, HEAD_PAIRS - 2)
+        first_product(1, HEAD_PAIRS - 1)
 
-        first_product(1, 0)
-        transpose_v(0)
-        transpose_v(1)
+        slabs = {5: [(0, 0), (0, 1)], 6: [(0, 2), (0, 3)], 7: [(1, 0), (1, 1)]}
+        for bank in range(4):
+            transpose_v(bank)
         for step in range(STEPS):
-            if step < STEPS // 2:
-                for pair in (2 * step + 1, 2 * step + 2):
-                    if pair < HEAD_PAIRS:
-                        first_product(1, pair)
-            else:
-                tile_index, chunk_pair = divmod(step - STEPS // 2, 2)
-                second_product(tile_index, 2 * chunk_pair)
-                second_product(tile_index, 2 * chunk_pair + 1)
-            mix_and_norm(step)
-            if step + 1 < STEPS:
-                transpose_v(2 * step + 2)
-                transpose_v(2 * step + 3)
+            for tile_index, chunk in slabs.get(step, []):
+                second_product(tile_index, chunk)
+            mix_and_norm(step, [(1, 2), (1, 3)] if step == STEPS - 1 else [])
+            for bank in (2 * step + 4, 2 * step + 5):
+                if bank < MIX_BANKS:
+                    transpose_v(bank)
         for tile_index in range(TOKEN_TILES // 2, TOKEN_TILES):
             for chunk in range(N_CHUNKS):
                 second_product(tile_index, chunk)

@@ -56,6 +56,8 @@ def tile_differentialattention_pb_kernel(
         psum = ctx.enter_context(tc.psum_pool(name="psum", bufs=PSUM_BANKS))
         ctx.enter_context(tc.manual_schedule())
 
+        zeros = const.tile([P, BANK], BF16)
+        nc.vector.memset(zeros[:], 0.0)
         wv_planes = const.tile([P, WIDTH], U8, align_bytes=64)
         wo_planes = const.tile([P, WIDTH], U8, align_bytes=64)
         nc.vector.memset(wv_planes[:].bitcast(I32), 0)
@@ -79,13 +81,22 @@ def tile_differentialattention_pb_kernel(
             op=ALU.add,
         )
 
+        unread = psum.tile([P, BANK], F32, tag="bank")
+
+        def keep_clock_up(count):
+            for n in range(count):
+                nc.tensor.matmul(out=unread[:], lhsT=zeros[:, 0:P], rhs=zeros[:], start=True, stop=True)
+
         x_sb = {}
 
         def load_x(tile_index):
             x_sb[tile_index] = keep.tile([P, WIDTH], BF16, name="x_sb", tag="x_sb", bufs=TOKEN_TILES)
-            nc.sync.dma_start(
-                out=x_sb[tile_index][:], in_=x_rows[tile_index * P : (tile_index + 1) * P, :]
-            )
+            for part in range(2):
+                cols = slice(part * WIDTH // 2, (part + 1) * WIDTH // 2)
+                nc.sync.dma_start(
+                    out=x_sb[tile_index][:, cols],
+                    in_=x_rows[tile_index * P : (tile_index + 1) * P, cols],
+                )
 
         def load_scale_planes(planes, scales):
             rows = scales.bitcast(I32)
@@ -148,6 +159,7 @@ def tile_differentialattention_pb_kernel(
                         out=grouped_words[:, 2 * g_pair : 2 * g_pair + 2, i * P : (i + 1) * P, :],
                         in_=xt[:].rearrange("p g u t -> p g t u"),
                     )
+                keep_clock_up(1)
             x_codes[half] = keep.tile([P, PASSES, HALF], U32, name="x_codes%d" % half, align_bytes=64)
             x_scales[half] = keep.tile([P, PASSES, HALF], U8, name="x_scales%d" % half, align_bytes=64)
             nc.vector.quantize_mx(
@@ -342,6 +354,7 @@ def tile_differentialattention_pb_kernel(
                 for chunk in range(N_CHUNKS)
             ]
         )
+        keep_clock_up(5)
         quantise_x(0)
         quantise_x(1)
         order_diff()

@@ -308,7 +308,7 @@ def tile_differentialattention_pb_kernel(
                 .bitcast(F32)
                 .rearrange("p (g a t jp) -> p g a t jp", g=PASSES, a=GROUPS_PER_TILE, jp=2)
             )
-            nc.vector.tensor_copy(
+            nc.gpsimd.tensor_copy(
                 out=grouped_words[:, :, first : first + 2 * GROUPS_PER_BANK, :, :],
                 in_=r_cols[:]
                 .bitcast(F32)

import math
from contextlib import ExitStack

import concourse.mybir as mybir
from concourse.masks import make_identity

F32 = mybir.dt.float32
BF16 = mybir.dt.bfloat16
I32 = mybir.dt.int32
U32 = mybir.dt.uint32
U8 = mybir.dt.uint8
FP8X4 = mybir.dt.float8_e4m3fn_x4
ACT = mybir.ActivationFunctionType
ALU = mybir.AluOpType

P = 128
PACK = 4
PASSES = 4
TOKENS = 512
WIDTH = 2048
HEADS = 16
HEAD_DIM = 128
BANK = 512
PSUM_BANKS = 8
N_CHUNKS = WIDTH // BANK
TOKEN_TILES = TOKENS // P
HALF = TOKENS // 2
HEAD_PAIRS = HEADS // 2

GROUP_TOKENS = 8
GROUPS = TOKENS // GROUP_TOKENS
GROUPS_PER_BANK = BANK // HEAD_DIM
MIX_BANKS = GROUPS // GROUPS_PER_BANK
GROUPS_PER_TILE = GROUPS // TOKEN_TILES
STEPS = MIX_BANKS // 2
STEPS_PER_TILE = STEPS // TOKEN_TILES

L0 = 0.8 - 0.6 * math.exp(-0.3 * 12)
KEEP = 1.0 - L0
EPS = 1e-5

FLOPS = 2 * 2 * TOKENS * WIDTH * WIDTH + 2 * TOKENS * HEADS * HEADS * HEAD_DIM


def tile_differentialattention_pb_kernel(
    tc, x, diff, Wv_words, Wv_scales, Wo_words, Wo_scales, bo, out
):
    nc = tc.nc
    x_rows = x.flatten_outer_dims()
    out_rows = out.flatten_outer_dims()

    with ExitStack() as ctx:
        const = ctx.enter_context(tc.tile_pool(name="const", bufs=1))
        keep = ctx.enter_context(tc.tile_pool(name="keep", bufs=1))
        work = ctx.enter_context(tc.tile_pool(name="work", bufs=3))
        psum = ctx.enter_context(tc.psum_pool(name="psum", bufs=PSUM_BANKS))
        ctx.enter_context(tc.manual_schedule())

        zeros = const.tile([P, BANK], BF16)
        nc.vector.memset(zeros[:], 0.0)
        wv_planes = const.tile([P, WIDTH], U8, align_bytes=64)
        wo_planes = const.tile([P, WIDTH], U8, align_bytes=64)
        nc.vector.memset(wv_planes[:].bitcast(I32), 0)
        nc.vector.memset(wo_planes[:].bitcast(I32), 0)

        ident_f32 = const.tile([P, P], F32)
        make_identity(nc, ident_f32[:])
        ident_bf16 = const.tile([P, P], BF16)
        make_identity(nc, ident_bf16[:])

        one = const.tile([P, 1], F32)
        nc.vector.memset(one[:], 1.0)
        one_root = const.tile([P, 1], F32)
        nc.scalar.activation(out=one_root[:], in_=one[:], func=ACT.Sqrt)

        same_token = const.tile([P, GROUP_TOKENS], F32)
        nc.vector.tensor_reduce(
            out=same_token[:],
            in_=ident_f32[:].rearrange("k (h t) -> k t h", h=HEADS),
            axis=mybir.AxisListType.X,
            op=ALU.add,
        )

        unread = psum.tile([P, BANK], F32, tag="bank")

        def keep_clock_up(count):
            for n in range(count):
                nc.tensor.matmul(out=unread[:], lhsT=zeros[:, 0:P], rhs=zeros[:], start=True, stop=True)

        x_sb = {}

        def load_x(tile_index):
            x_sb[tile_index] = keep.tile([P, WIDTH], BF16, name="x_sb", tag="x_sb", bufs=TOKEN_TILES)
            for part in range(2):
                cols = slice(part * WIDTH // 2, (part + 1) * WIDTH // 2)
                nc.sync.dma_start(
                    out=x_sb[tile_index][:, cols],
                    in_=x_rows[tile_index * P : (tile_index + 1) * P, cols],
                )

        def load_scale_planes(planes, scales):
            rows = scales.bitcast(I32)
            for quadrant in range(4):
                nc.sync.dma_start(
                    out=planes[32 * quadrant : 32 * quadrant + 16, :].bitcast(I32),
                    in_=rows[:, 4 * quadrant : 4 * quadrant + 4, :],
                )

        def load_weight_columns(words, first, count, name):
            view = words.rearrange("g p n j -> g p (n j)").bitcast(I32).rearrange("g p n -> p g n")
            w = keep.tile([P, PASSES, count], U32, name=name, align_bytes=64)
            nc.sync.dma_start(out=w[:].bitcast(I32), in_=view[:, :, first : first + count])
            return w

        def load_wv(pair):
            return load_weight_columns(Wv_words, pair * 2 * HEAD_DIM, 2 * HEAD_DIM, "wv%d" % pair)

        diff_rows = keep.tile([P, GROUP_TOKENS, 8, HEADS], BF16)
        diff_view = diff.rearrange("b n a h -> (b n) a h").rearrange(
            "(a t) (s e) h -> s a t (e h)", t=GROUP_TOKENS, s=2
        )

        def load_diff():
            for s in range(2):
                nc.sync.dma_start(
                    out=diff_rows[64 * s : 64 * (s + 1), :, :, :].rearrange("q t e h -> q t (e h)"),
                    in_=diff_view[s],
                )

        bias = const.tile([P, WIDTH], BF16)
        wv = []
        wo = []

        x_codes = {}
        x_scales = {}

        def quantise_x(half):
            grouped = keep.tile([P, PASSES, HALF, PACK], BF16, tag="x_grouped", bufs=2, align_bytes=64)
            grouped_words = (
                grouped[:]
                .rearrange("p g t j -> p (g t j)")
                .bitcast(F32)
                .rearrange("p (g t u) -> p g t u", g=PASSES, u=2)
            )
            for i in range(2):
                x_words = x_sb[2 * half + i][:].bitcast(F32)
                for g_pair in range(2):
                    xt = psum.tile([P, 2, 2, P], F32, tag="bank")
                    for gi in range(2):
                        g = 2 * g_pair + gi
                        for u in range(2):
                            nc.tensor.transpose(
                                xt[:, gi, u, :],
                                x_words[:, 256 * g + u : 256 * (g + 1) : 2],
                                ident_f32[:],
                            )
                    copy = nc.vector.tensor_copy if g_pair == 0 else nc.scalar.copy
                    copy(
                        out=grouped_words[:, 2 * g_pair : 2 * g_pair + 2, i * P : (i + 1) * P, :],
                        in_=xt[:].rearrange("p g u t -> p g t u"),
                    )
                keep_clock_up(1)
            x_codes[half] = keep.tile([P, PASSES, HALF], U32, name="x_codes%d" % half, align_bytes=64)
            x_scales[half] = keep.tile([P, PASSES, HALF], U8, name="x_scales%d" % half, align_bytes=64)
            nc.vector.quantize_mx(
                out=x_codes[half][:].rearrange("p g t -> p (g t)").bitcast(FP8X4),
                scales=x_scales[half][:].rearrange("p g t -> p (g t)"),
                in_=grouped[:].rearrange("p g t j -> p (g t j)"),
            )

        v_t = keep.tile([P, GROUPS, HEADS, GROUP_TOKENS], F32)

        def first_product(half, pair):
            acc = psum.tile([P, 2, HALF], F32, tag="bank")
            for i in range(2):
                head = 2 * pair + i
                for g in range(PASSES):
                    nc.tensor.matmul_mx(
                        out=acc[:, i, :],
                        lhsT=wv[pair][:, g, i * P : (i + 1) * P].bitcast(FP8X4),
                        lhsT_scale=wv_planes[4 * g : P, head * P : (head + 1) * P],
                        rhs=x_codes[half][:, g, :].bitcast(FP8X4),
                        rhs_scale=x_scales[half][:, g, :],
                        start=(g == 0),
                        stop=(g == PASSES - 1),
                    )
            groups = slice(half * GROUPS // 2, (half + 1) * GROUPS // 2)
            copy = nc.vector.tensor_copy if half == 1 else nc.scalar.copy
            copy(
                out=v_t[:, groups, 2 * pair : 2 * pair + 2, :],
                in_=acc[:].rearrange("d i (a t) -> d a i t", t=GROUP_TOKENS),
            )

        mixer = keep.tile([P, GROUPS, HEADS, GROUP_TOKENS], F32)
        diff_t = keep.tile([P, GROUPS, 4, 4], F32)

        diff_cols = keep.tile([P, 8, HEADS, GROUP_TOKENS], BF16)

        def order_diff():
            nc.vector.tensor_copy(out=diff_cols[:], in_=diff_rows[:].rearrange("q t e h -> q e h t"))

        def transpose_diff():
            diff_tp = psum.tile([P, 8, P], BF16, tag="bank")
            for e in range(8):
                nc.tensor.transpose(
                    diff_tp[:, e, :],
                    diff_cols[:, e, :, :].rearrange("q h t -> q (h t)"),
                    ident_bf16[:],
                )
            nc.vector.tensor_copy(
                out=diff_t[:].rearrange("k a lo (s f) -> k a lo s f", s=2),
                in_=diff_tp[:].rearrange("k (f lo) (s a) -> k a lo s f", f=2, s=2),
            )

        def build_mixer(tile_index):
            groups = slice(tile_index * GROUPS_PER_TILE, (tile_index + 1) * GROUPS_PER_TILE)
            shape = [P, GROUPS_PER_TILE * HEADS, GROUP_TOKENS]
            nc.vector.tensor_tensor(
                out=mixer[:, groups, :, :].rearrange("k a m t -> k (a m) t"),
                in0=diff_t[:, groups, :, :]
                .rearrange("k a lo hi -> k (a lo hi)")
                .unsqueeze(2)
                .to_broadcast(shape),
                in1=same_token[:].unsqueeze(1).to_broadcast(shape),
                op=ALU.mult,
            )

        r_codes = keep.tile([P, TOKEN_TILES, PASSES * P], U32, align_bytes=64)
        r_scales = keep.tile([P, TOKEN_TILES, PASSES * P], U8, align_bytes=64)
        v_groups = {}
        r_grouped = {}

        def transpose_v(bank):
            v_tp = psum.tile([P, GROUPS_PER_BANK, HEAD_DIM], F32, tag="bank")
            for i in range(GROUPS_PER_BANK):
                nc.tensor.transpose(
                    v_tp[:, i, :],
                    v_t[:, bank * GROUPS_PER_BANK + i, :, :].rearrange("d h t -> d (h t)"),
                    ident_f32[:],
                )
            v_g = work.tile([P, GROUPS_PER_BANK, 2, 32, 2], F32, tag="v_g", bufs=6)
            nc.scalar.copy(
                out=v_g[:], in_=v_tp[:].rearrange("k i (q jp j2) -> k i jp q j2", jp=2, j2=2)
            )
            v_groups[bank] = v_g

        def mix_and_norm(step, behind_mix=()):
            tile_index, step_in_tile = divmod(step, STEPS_PER_TILE)
            mixed = []
            for bank in (2 * step, 2 * step + 1):
                mixed.append(psum.tile([P, GROUPS_PER_BANK, HEAD_DIM], F32, name="mixed", tag="bank"))
                for i in range(GROUPS_PER_BANK):
                    nc.tensor.matmul(
                        out=mixed[-1][:, i, :],
                        lhsT=mixer[:, bank * GROUPS_PER_BANK + i, :, :].rearrange("k m t -> k (m t)"),
                        rhs=v_groups[bank][:, i, :, :, :].rearrange("k jp q j2 -> k (jp q j2)"),
                        start=True,
                        stop=True,
                    )
            for out_tile, chunk in behind_mix:
                second_product(out_tile, chunk)
            squares = work.tile([P, 2, GROUPS_PER_BANK, HEAD_DIM], BF16, tag="squares", bufs=1)
            sum_sq = work.tile([P, 2, GROUPS_PER_BANK], F32, tag="sum_sq")
            for b in range(2):
                for i in range(GROUPS_PER_BANK):
                    nc.scalar.activation(
                        out=squares[:, b, i, :],
                        in_=mixed[b][:, i, :],
                        func=ACT.Square,
                        accum_out=sum_sq[:, b, i : i + 1],
                    )
            root = work.tile([P, 2, GROUPS_PER_BANK], F32, tag="root")
            nc.scalar.activation(
                out=root[:],
                in_=sum_sq[:],
                func=ACT.Sqrt,
                scale=1.0 / (HEAD_DIM * KEEP * KEEP),
                bias=EPS / (KEEP * KEEP),
            )
            gain = work.tile([P, 2, GROUPS_PER_BANK], F32, tag="gain")
            nc.vector.reciprocal(out=gain[:], in_=root[:])
            r_rows = work.tile([P, 2, GROUPS_PER_BANK, HEAD_DIM], BF16, tag="r_rows", bufs=2, align_bytes=64)
            for b in range(2):
                nc.vector.tensor_tensor(
                    out=r_rows[:, b, :, :],
                    in0=mixed[b][:],
                    in1=gain[:, b, :].unsqueeze(2).to_broadcast([P, GROUPS_PER_BANK, HEAD_DIM]),
                    op=ALU.mult,
                )
            r_cols = work.tile([P, 2 * BANK], BF16, tag="r_cols", align_bytes=64)
            nc.vector.transpose(
                out=r_cols[:].bitcast(F32),
                in_=r_rows[:].rearrange("m b i c -> m (b i c)").bitcast(F32),
            )
            if step_in_tile == 0:
                r_grouped[tile_index] = work.tile(
                    [P, PASSES, GROUPS_PER_TILE, GROUP_TOKENS, PACK],
                    BF16,
                    name="r_grouped",
                    tag="r_grouped",
                    bufs=2,
                    align_bytes=64,
                )
            first = step_in_tile * 2 * GROUPS_PER_BANK
            grouped_words = (
                r_grouped[tile_index][:]
                .rearrange("p g a t j -> p (g a t j)")
                .bitcast(F32)
                .rearrange("p (g a t jp) -> p g a t jp", g=PASSES, a=GROUPS_PER_TILE, jp=2)
            )
            nc.gpsimd.tensor_copy(
                out=grouped_words[:, :, first : first + 2 * GROUPS_PER_BANK, :, :],
                in_=r_cols[:]
                .bitcast(F32)
                .rearrange("p (a jp hi t) -> p hi a t jp", a=2 * GROUPS_PER_BANK, jp=2, hi=PASSES),
            )
            if step_in_tile == STEPS_PER_TILE - 1:
                nc.vector.quantize_mx(
                    out=r_codes[:, tile_index, :].bitcast(FP8X4),
                    scales=r_scales[:, tile_index, :],
                    in_=r_grouped[tile_index][:].rearrange("p g a t j -> p (g a t j)"),
                )

        def second_product(tile_index, chunk):
            cols = slice(chunk * BANK, (chunk + 1) * BANK)
            acc = psum.tile([P, BANK], F32, tag="bank")
            for g in range(PASSES):
                nc.tensor.matmul_mx(
                    out=acc[:],
                    lhsT=r_codes[:, tile_index, g * P : (g + 1) * P].bitcast(FP8X4),
                    lhsT_scale=r_scales[:, tile_index, g * P : (g + 1) * P],
                    rhs=wo[chunk][:, g, :].bitcast(FP8X4),
                    rhs_scale=wo_planes[4 * g : P, cols],
                    start=(g == 0),
                    stop=(g == PASSES - 1),
                )
            result = work.tile([P, BANK], F32, tag="result", bufs=4)
            nc.vector.tensor_tensor(out=result[:], in0=acc[:], in1=bias[:, cols], op=ALU.add)
            nc.sync.dma_start(
                out=out_rows[tile_index * P : (tile_index + 1) * P, cols], in_=result[:]
            )

        for tile_index in range(TOKEN_TILES):
            load_x(tile_index)
        load_scale_planes(wv_planes, Wv_scales)
        wv.extend([load_wv(pair) for pair in range(2)])
        load_diff()
        wv.extend([load_wv(pair) for pair in range(2, HEAD_PAIRS)])
        nc.sync.dma_start(out=bias[:], in_=bo.partition_broadcast(P))
        load_scale_planes(wo_planes, Wo_scales)
        wo.extend(
            [
                load_weight_columns(Wo_words, chunk * BANK, BANK, "wo%d" % chunk)
                for chunk in range(N_CHUNKS)
            ]
        )
        keep_clock_up(5)
        quantise_x(0)
        quantise_x(1)
        order_diff()
        for pair in range(2):
            first_product(0, pair)
        for pair in range(2):
            first_product(1, pair)
        first_product(0, 2)
        transpose_diff()
        first_product(1, 2)
        for pair in range(3, HEAD_PAIRS - 2):
            first_product(0, pair)
            first_product(1, pair)
            build_mixer(pair - 3)
        first_product(0, HEAD_PAIRS - 2)
        first_product(0, HEAD_PAIRS - 1)
        build_mixer(3)
        first_product(1, HEAD_PAIRS - 2)
        first_product(1, HEAD_PAIRS - 1)

        slabs = {5: [(0, 0), (0, 1)], 6: [(0, 2), (0, 3)], 7: [(1, 0), (1, 1)]}
        for bank in range(4):
            transpose_v(bank)
        for step in range(STEPS):
            for tile_index, chunk in slabs.get(step, []):
                second_product(tile_index, chunk)
            mix_and_norm(step, [(1, 2), (1, 3)] if step == STEPS - 1 else [])
            for bank in (2 * step + 4, 2 * step + 5):
                if bank < MIX_BANKS:
                    transpose_v(bank)
        for tile_index in range(TOKEN_TILES // 2, TOKEN_TILES):
            for chunk in range(N_CHUNKS):
                second_product(tile_index, chunk)
